import numpy as np
import ml_dtypes


def mxq(x, axis, fmt="e4m3"):
    dtype, down = {"e4m3": (ml_dtypes.float8_e4m3fn, 7), "e5m2": (ml_dtypes.float8_e5m2, 14)}[fmt]
    v = np.moveaxis(np.asarray(x, np.float32).astype(ml_dtypes.bfloat16).astype(np.float64), axis, -1)
    blocks = v.reshape(v.shape[:-1] + (-1, 32))
    amax = np.abs(blocks).max(-1, keepdims=True)
    byte = np.maximum(np.where(amax > 0, np.frexp(amax)[1] - 1 + 127, 0) - down, 1)
    scale = np.exp2(byte - 127.0)
    codes = (blocks / scale).astype(np.float32).astype(dtype).astype(np.float64)
    return np.moveaxis((codes * scale).reshape(v.shape), -1, axis)


WIDE = False


def mx_kscale(k):
    if not WIDE:
        return np.ones(k)
    levels = np.array([10, -10, 5, -5, 0])
    if k % 512:
        return np.exp2(np.random.permutation(np.resize(levels, k // 32))).repeat(32)
    a = np.empty((k // 512, 16))
    for p in range(k // 512):
        a[p, :8] = np.random.permutation(np.resize(levels, 8))
        for g in range(8):
            far = levels[np.abs(levels - a[p, g]) >= 10]
            a[p, g + 8] = far[np.random.randint(len(far))]
    return np.exp2(a.ravel()).repeat(32)


BF16 = ml_dtypes.bfloat16


def bf(x):
    return np.asarray(x, np.float32).astype(BF16)


def f64(x):
    return np.asarray(x).astype(np.float64)


E2M1 = np.array([0.0, 0.5, 1.0, 1.5, 2.0, 3.0, 4.0, 6.0, -0.0, -0.5, -1.0, -1.5, -2.0, -3.0, -4.0, -6.0])


def pack_weight(w, fmt):
    k, n = w.shape
    w = f64(bf(w)).reshape(k // 32, 32, n)
    amax = np.abs(w).max(1)
    if fmt == "e4m3":
        byte = np.frexp(amax)[1] - 1 + 127 - 7
    else:
        mant, ex = np.frexp(amax / 6.0)
        byte = np.where(mant > 0.5, ex, ex - 1) + 127
    byte = np.clip(np.where(amax > 0, byte, 1), 1, 254)
    scaled = (w * np.exp2(127.0 - byte)[:, None, :]).reshape(k, n).astype(np.float32)
    by_word = np.ascontiguousarray(scaled.reshape(k // 512, 128, 4, n).transpose(0, 1, 3, 2))
    if fmt == "e4m3":
        words = by_word.astype(ml_dtypes.float8_e4m3fn).view(np.uint8)
    else:
        c = by_word.astype(ml_dtypes.float4_e2m1fn).view(np.uint8) & 0xF
        words = c[..., 0::2] | (c[..., 1::2] << 4)
    return np.ascontiguousarray(words), np.ascontiguousarray(byte.astype(np.uint8).reshape(k // 512, 16, n))


def unpack_weight(words, scales, fmt):
    g, p, n, _ = words.shape
    if fmt == "e4m3":
        vals = np.ascontiguousarray(words).view(ml_dtypes.float8_e4m3fn).astype(np.float64)
    else:
        nib = np.empty((g, p, n, 4), np.uint8)
        nib[..., 0::2] = words & 0xF
        nib[..., 1::2] = words >> 4
        vals = E2M1[nib]
    vals = vals * np.repeat(np.exp2(scales.astype(np.float64) - 127.0), 8, axis=1)[..., None]
    return vals.transpose(0, 1, 3, 2).reshape(g * 512, n)


N, C, T, V, IC = 4, 1024, 8, 128, 512
G = (IC * T) ** 0.25


def draw0():
    s = mx_kscale(C)
    u = mx_kscale(IC * T)[::T]
    x = bf(np.random.standard_normal((N, C, T, V)) * s[None, :, None, None])
    Wa = np.random.standard_normal((IC, C)) * G / np.sqrt(C) / s[None, :] * u[:, None]
    Wa_words, Wa_scales = pack_weight(Wa.T, "e4m3")
    ba = bf(np.random.standard_normal(IC) * 0.3 * G * u)
    Wb = np.random.standard_normal((IC, C)) * G / np.sqrt(C) / s[None, :] / u[:, None]
    Wb_words, Wb_scales = pack_weight(Wb.T, "e4m3")
    return {"x": x,
            "Wa_words": Wa_words,
            "Wa_scales": Wa_scales,
            "ba": ba,
            "Wb_words": Wb_words,
            "Wb_scales": Wb_scales,
            "bb": bf(np.random.standard_normal(IC) * 0.3 * G / u),
            "A": bf(np.eye(V)[None] + 0.1 * np.random.standard_normal((1, V, V))),
            "alpha": bf(2.0 + 0.2 * np.random.standard_normal(1))}


def core(x, Wa_words, Wa_scales, ba, Wb_words, Wb_scales, bb, A, alpha):
    n, c, t, v = x.shape
    ic = Wa_words.shape[2]
    xq = mxq(f64(x), 1, "e4m3").reshape(n, c, t * v)
    qa = (unpack_weight(Wa_words, Wa_scales, "e4m3").T @ xq).reshape(n, ic, t, v) + f64(ba)[None, :, None, None]
    kb = (unpack_weight(Wb_words, Wb_scales, "e4m3").T @ xq).reshape(n, ic, t, v) + f64(bb)[None, :, None, None]
    Q = qa.transpose(0, 3, 1, 2).reshape(n, v, ic * t)
    K = kb.reshape(n, ic * t, v)
    Graph_B = np.tanh((mxq(Q, 2, "e4m3") @ mxq(K, 1, "e4m3")) / (ic * t))
    z = f64(A) + Graph_B * f64(alpha)
    e = np.exp(z - z.max(-1, keepdims=True))
    return e / e.sum(-1, keepdims=True)


def e4m3fn_bytes(y):
    return np.clip(np.asarray(y, np.float64), -448.0, 448.0).astype(np.float32).astype(ml_dtypes.float8_e4m3fn).view(np.uint8)


def e4m3fn_values(b):
    return np.asarray(b, np.uint8).view(ml_dtypes.float8_e4m3fn).astype(np.float64)


def setup_inputs():
    d = draw0()
    x0 = np.asarray(d['x']).astype(np.float64)
    s = (np.max(np.abs(x0), axis=(0, 2, 3), keepdims=True) / 448.0).astype(np.float32)
    out = {}
    for k, v in d.items():
        if k == 'x':
            out['x_bytes'] = e4m3fn_bytes(x0 / s.astype(np.float64))
            out['x_scale'] = s
        else:
            out[k] = v
    return out


def reference(x_bytes, x_scale, Wa_words, Wa_scales, ba, Wb_words, Wb_scales, bb, A, alpha):
    return core(e4m3fn_values(x_bytes) * x_scale.astype(np.float64), Wa_words, Wa_scales, ba, Wb_words, Wb_scales, bb, A, alpha)

@@ -1,0 +1,279 @@
+from contextlib import ExitStack
+
+import concourse.mybir as mybir
+from concourse.masks import make_identity
+
+N, C, T, V, IC = 4, 1024, 8, 128, 512
+F32 = mybir.dt.float32
+BF16 = mybir.dt.bfloat16
+U32 = mybir.dt.uint32
+I32 = mybir.dt.int32
+U8 = mybir.dt.uint8
+FP8 = mybir.dt.float8_e4m3fn
+FP8X4 = mybir.dt.float8_e4m3fn_x4
+ACT = mybir.ActivationFunctionType
+ALU = mybir.AluOpType
+AX = mybir.AxisListType
+
+FLOPS = 2 * 2 * N * IC * C * T * V + N * 2 * V * V * IC * T
+
+P = 128
+H = 512
+
+
+def tile_adaptivegraphconstruction_t_w8_kernel(
+    tc, x_bytes, x_scale, Wa_words, Wa_scales, ba, Wb_words, Wb_scales, bb, A, alpha, out
+):
+    nc = tc.nc
+    with ExitStack() as ctx:
+        keep = ctx.enter_context(tc.tile_pool(name="keep", bufs=1))
+        xb_pool = ctx.enter_context(tc.tile_pool(name="xb", bufs=8))
+        pl_pool = ctx.enter_context(tc.tile_pool(name="plp", bufs=6))
+        gr_pool = ctx.enter_context(tc.tile_pool(name="grp", bufs=4))
+        codes = ctx.enter_context(tc.tile_pool(name="codes", bufs=6))
+        ypool = ctx.enter_context(tc.tile_pool(name="yp", bufs=4))
+        xpool = ctx.enter_context(tc.tile_pool(name="xp", bufs=8))
+        small = ctx.enter_context(tc.tile_pool(name="small", bufs=2))
+        psum = ctx.enter_context(tc.psum_pool(name="psum", bufs=6))
+        psum2 = ctx.enter_context(tc.psum_pool(name="psum2", bufs=2))
+        ctx.enter_context(tc.manual_schedule())
+
+        xs = keep.tile([P, 8], F32, name="xs")
+        nc.scalar.dma_start(
+            out=xs[:].rearrange("p (g j) -> p g j", j=4),
+            in_=x_scale.rearrange("o (g p j) a b -> p (o g) (j a b)", p=P, j=4),
+        )
+        xbs = {}
+        for n in range(N):
+            for g in range(2):
+                xbs[n, g] = xb_pool.tile([P, 4, 2, H], U8, name="xb")
+
+        def load(n, g, ths):
+            src = x_bytes[n, 512 * g : 512 * (g + 1)].rearrange("(p j) (h t) v -> p j h (t v)", j=4, h=2)
+            if len(ths) == 2:
+                nc.sync.dma_start(
+                    out=xbs[n, g][:].rearrange("p j h w -> p (j h w)"), in_=src.rearrange("p j h w -> p (j h w)")
+                )
+            else:
+                nc.sync.dma_start(out=xbs[n, g][:, :, ths[0], :], in_=src[:, :, ths[0], :])
+
+        load(0, 0, [0])
+        load(0, 1, [0])
+
+        wsc = keep.tile([P, IC], U8, name="wsc", align_bytes=64)
+        nc.vector.memset(wsc[:].bitcast(I32), 0)
+        dummy = keep.tile([P, 1], F32, name="dummy")
+        nc.vector.memset(dummy[:], 0.0)
+        brow = keep.tile([P, P], BF16, name="brow", align_bytes=64)
+        nc.vector.memset(brow[:], 0.0)
+        nc.scalar.activation(out=dummy[:], in_=dummy[:], func=ACT.Tanh)
+        for op, src in enumerate((Wa_scales, Wb_scales)):
+            for q in range(4):
+                r = 32 * q + 8 * op
+                nc.sync.dma_start(out=wsc[r : r + 8, :].bitcast(I32), in_=src[:, 4 * q : 4 * q + 4, :].bitcast(I32))
+        wcodes = []
+        for op, src in enumerate((Wa_words, Wb_words)):
+            w = keep.tile([P, 2, IC * 4], U8, name="w%d" % op, align_bytes=64)
+            nc.sync.dma_start(out=w[:], in_=src.rearrange("g p n t -> p g (n t)"))
+            wcodes.append(w)
+        load(0, 0, [1])
+        load(0, 1, [1])
+
+        ident = keep.tile([P, P], BF16, name="ident", align_bytes=64)
+        make_identity(nc, ident[:])
+        nc.scalar.dma_start(out=brow[0:4, :], in_=ba.rearrange("(m p) -> m p", p=P))
+        nc.scalar.dma_start(out=brow[4:8, :], in_=bb.rearrange("(m p) -> m p", p=P))
+        a_raw = keep.tile([P, V], BF16, name="a_raw")
+        nc.scalar.dma_start(out=a_raw[:], in_=A[0])
+        al_raw = keep.tile([P, 1], BF16, name="al_raw")
+        nc.scalar.dma_start(out=al_raw[:], in_=alpha.partition_broadcast(P))
+        for n in range(1, N):
+            load(n, 0, [0, 1])
+            load(n, 1, [0, 1])
+
+        planes = {}
+        grouped = {}
+        xq = {}
+        units = [(n, th) for n in range(N) for th in range(2)]
+        s_share = [4, 6, 3, 3, 3, 3, 3, 2]
+
+        def on_scalar(u, g, j):
+            return j < (s_share[u] + 1 - g) // 2
+
+        def widen(u, g, j):
+            n, th = units[u]
+            if (u, g) not in planes:
+                planes[u, g] = pl_pool.tile([P, 4, H], BF16, name="planes", align_bytes=64)
+            src = xbs[n, g][:, j, th, :].bitcast(FP8)
+            dst = planes[u, g][:, j, :]
+            sc = xs[:, 4 * g + j : 4 * g + j + 1]
+            if on_scalar(u, g, j):
+                nc.scalar.activation(out=dst, in_=src, func=ACT.Copy, scale=sc)
+            else:
+                nc.vector.tensor_scalar(out=dst, in0=src, scalar1=sc, scalar2=None, op0=ALU.mult)
+
+        def widen_on(u, scalar):
+            return [(u, g, j) for g in range(2) for j in range(4) if on_scalar(u, g, j) == scalar]
+
+        def interleave(u, g):
+            t = gr_pool.tile([P, H, 4], BF16, name="grouped", align_bytes=64)
+            grouped[u, g] = t
+            nc.vector.tensor_copy(
+                out=t[:].rearrange("p (c i) j -> p c j i", i=4),
+                in_=planes[u, g][:].rearrange("p j (c i) -> p c j i", i=4),
+            )
+
+        def quant(u, g):
+            cw = codes.tile([P, H], U32, name="cw", align_bytes=64)
+            cs = codes.tile([P, H], U8, name="cs", align_bytes=64)
+            nc.vector.quantize_mx(
+                out=cw[:].bitcast(FP8X4), scales=cs[:], in_=grouped[u, g][:].rearrange("p w j -> p (w j)")
+            )
+            xq[u, g] = (cw, cs)
+
+        ys = {}
+        xt = {}
+
+        def project(u, m, op):
+            n, th = units[u]
+            if op == 0:
+                ys[u, m] = ypool.tile([P, 2, H], BF16, name="y", align_bytes=64)
+            bank = psum.tile([P, H], F32, name="bank")
+            for g in range(2):
+                cw, cs = xq[u, g]
+                nc.tensor.matmul_mx(
+                    out=bank[:],
+                    lhsT=wcodes[op][:, g, 512 * m : 512 * (m + 1)].bitcast(FP8X4),
+                    lhsT_scale=wsc[4 * (2 * op + g) : P, 128 * m : 128 * (m + 1)],
+                    rhs=cw[:].bitcast(FP8X4),
+                    rhs_scale=cs[:],
+                    start=(g == 0),
+                    stop=(g == 1),
+                )
+            dst = ys[u, m][:, op, :].rearrange("p (v j) -> p v j", j=4)
+            src = bank[:].rearrange("p (j v) -> p v j", j=4)
+            b = bias[:, 4 * op + m : 4 * op + m + 1]
+            if u == len(units) - 1 and op == 1:
+                nc.vector.tensor_scalar(out=dst, in0=src, scalar1=b, scalar2=None, op0=ALU.add)
+            else:
+                nc.scalar.activation(out=dst, in_=src, func=ACT.Identity, bias=b)
+
+        def swap(u, m):
+            n, th = units[u]
+            if th == 0:
+                xt[n, m] = xpool.tile([P, 2, 2 * H], BF16, name="xt", align_bytes=64)
+            for hh in range(2):
+                nc.sync.dma_start(
+                    out=xt[n, m][th:P:2, hh, :],
+                    in_=ys[u, m][64 * hh : 64 * hh + 64, :, :].rearrange("p o w -> p (o w)"),
+                )
+
+        qc = {}
+
+        def requant(n, m):
+            cw = codes.tile([P, 2, 2 * V], U32, name="ew", align_bytes=64)
+            cs = codes.tile([P, 2, 2 * V], U8, name="es", align_bytes=64)
+            nc.vector.quantize_mx(
+                out=cw[:].rearrange("p h w -> p (h w)").bitcast(FP8X4),
+                scales=cs[:].rearrange("p h w -> p (h w)"),
+                in_=xt[n, m][:].rearrange("p h w -> p (h w)"),
+            )
+            qc[n, m] = (cw, cs)
+
+        gps = {}
+
+        def product(n, m):
+            if m == 0:
+                gps[n] = psum2.tile([P, V], F32, name="gps")
+            cw, cs = qc[n, m]
+            for hh in range(2):
+                nc.tensor.matmul_mx(
+                    out=gps[n][:],
+                    lhsT=cw[:, hh, 0:V].bitcast(FP8X4),
+                    lhsT_scale=cs[:, hh, 0:V],
+                    rhs=cw[:, hh, V : 2 * V].bitcast(FP8X4),
+                    rhs_scale=cs[:, hh, V : 2 * V],
+                    start=(m == 0 and hh == 0),
+                    stop=(m == 3 and hh == 1),
+                )
+
+        def finish(n):
+            t = small.tile([P, V], F32, name="t")
+            nc.scalar.activation(out=t[:], in_=gps[n][:], func=ACT.Tanh, scale=1.0 / (IC * T))
+            nz = small.tile([P, V], F32, name="nz")
+            nc.vector.scalar_tensor_tensor(
+                out=nz[:], in0=t[:], scalar=neg_al[:, 0:1], in1=neg_a[:], op0=ALU.mult, op1=ALU.add
+            )
+            mn = small.tile([P, 1], F32, name="mn")
+            nc.vector.tensor_reduce(out=mn[:], in_=nz[:], axis=AX.X, op=ALU.min)
+            e = small.tile([P, V], F32, name="e")
+            tot = small.tile([P, 1], F32, name="tot")
+            nc.scalar.activation(out=e[:], in_=nz[:], func=ACT.Exp, scale=-1.0, bias=mn[:, 0:1], accum_out=tot[:])
+            rec = small.tile([P, 1], F32, name="rec")
+            nc.vector.reciprocal(out=rec[:], in_=tot[:])
+            o = small.tile([P, V], F32, name="o")
+            nc.vector.tensor_scalar(out=o[:], in0=e[:], scalar1=rec[:, 0:1], scalar2=None, op0=ALU.mult)
+            nc.sync.dma_start(out=out[n], in_=o[:])
+
+        for u in range(2):
+            for a in widen_on(u, True):
+                widen(*a)
+        for a in widen_on(0, False):
+            widen(*a)
+        interleave(0, 0)
+        interleave(0, 1)
+        quant(0, 0)
+        bias = keep.tile([P, 8], F32, name="bias")
+        tb = psum.tile([P, P], BF16, name="bank")
+        nc.tensor.transpose(tb[:], brow[:], ident[:])
+        nc.vector.tensor_copy(out=bias[:], in_=tb[:, 0:8])
+        quant(0, 1)
+        neg_a = keep.tile([P, V], F32, name="neg_a")
+        nc.vector.tensor_scalar(out=neg_a[:], in0=a_raw[:], scalar1=-1.0, scalar2=None, op0=ALU.mult)
+        neg_al = keep.tile([P, 1], F32, name="neg_al")
+        nc.vector.tensor_scalar(out=neg_al[:], in0=al_raw[:], scalar1=-1.0, scalar2=None, op0=ALU.mult)
+
+        last = len(units) - 1
+        ready = []
+        for u, (n, th) in enumerate(units):
+            s_work = widen_on(u + 2, True) if u + 2 <= last else []
+            todo = [(n - 1, 2 * th), (n - 1, 2 * th + 1)] if n > 0 else []
+            if u < last:
+                for a in widen_on(u + 1, False):
+                    widen(*a)
+                interleave(u + 1, 0)
+                if todo:
+                    requant(*todo[0])
+                interleave(u + 1, 1)
+                quant(u + 1, 0)
+                if todo:
+                    requant(*todo[1])
+                quant(u + 1, 1)
+            else:
+                for a in todo:
+                    requant(*a)
+            done = None
+            for k in range(8):
+                m, op = k // 2, k % 2
+                project(u, m, op)
+                if op == 1:
+                    swap(u, m)
+                if k in (1, 3, 5) and s_work:
+                    widen(*s_work.pop(0))
+                if k == 3:
+                    for a in ready:
+                        product(*a)
+                        if a[1] == 3:
+                            done = a[0]
+                    ready = todo
+            for a in s_work:
+                widen(*a)
+            if done is not None:
+                finish(done)
+        for a in ready:
+            product(*a)
+        finish(N - 2)
+        for m in range(4):
+            requant(N - 1, m)
+            product(N - 1, m)
+        finish(N - 1)

@@ -4,6 +4,7 @@ import concourse.mybir as mybir
 from concourse.masks import make_identity
 
 N, C, T, V, IC = 4, 1024, 8, 128, 512
+
 F32 = mybir.dt.float32
 BF16 = mybir.dt.bfloat16
 U32 = mybir.dt.uint32
@@ -18,7 +19,16 @@ AX = mybir.AxisListType
 FLOPS = 2 * 2 * N * IC * C * T * V + N * 2 * V * V * IC * T
 
 P = 128
-H = 512
+PACK = 4
+GROUPS = C // (P * PACK)
+COLS = T // 2 * V
+HALVES = 2 * N
+LAST = HALVES - 1
+QUARTERS = IC // P
+
+SCALAR_PLANES = [4, 6] + [2] * (HALVES - 2)
+VECTOR_BANKS = [(6, 4)]
+QUARTERS_BESIDE = [0, 0, 1, 1, 0, 2, 0, 0]
 
 
 def tile_adaptivegraphconstruction_t_w8_kernel(
@@ -27,253 +37,332 @@ def tile_adaptivegraphconstruction_t_w8_kernel(
     nc = tc.nc
     with ExitStack() as ctx:
         keep = ctx.enter_context(tc.tile_pool(name="keep", bufs=1))
-        xb_pool = ctx.enter_context(tc.tile_pool(name="xb", bufs=8))
-        pl_pool = ctx.enter_context(tc.tile_pool(name="plp", bufs=6))
-        gr_pool = ctx.enter_context(tc.tile_pool(name="grp", bufs=4))
-        codes = ctx.enter_context(tc.tile_pool(name="codes", bufs=6))
-        ypool = ctx.enter_context(tc.tile_pool(name="yp", bufs=4))
-        xpool = ctx.enter_context(tc.tile_pool(name="xp", bufs=8))
-        small = ctx.enter_context(tc.tile_pool(name="small", bufs=2))
+        first_bytes = ctx.enter_context(tc.tile_pool(name="first_bytes", bufs=2 * GROUPS))
+        more_bytes = ctx.enter_context(tc.tile_pool(name="more_bytes", bufs=(N - 1) * GROUPS))
+        plane_pool = ctx.enter_context(tc.tile_pool(name="plane_pool", bufs=3 * GROUPS))
+        group_pool = ctx.enter_context(tc.tile_pool(name="group_pool", bufs=2 * GROUPS))
+        codes = ctx.enter_context(tc.tile_pool(name="codes", bufs=3 * GROUPS))
+        row_pool = ctx.enter_context(tc.tile_pool(name="row_pool", bufs=HALVES * QUARTERS))
+        quarter_pool = ctx.enter_context(tc.tile_pool(name="quarter_pool", bufs=(N - 1) * QUARTERS))
+        ends = ctx.enter_context(tc.tile_pool(name="ends", bufs=N))
         psum = ctx.enter_context(tc.psum_pool(name="psum", bufs=6))
-        psum2 = ctx.enter_context(tc.psum_pool(name="psum2", bufs=2))
+        psum_g = ctx.enter_context(tc.psum_pool(name="psum_g", bufs=2))
         ctx.enter_context(tc.manual_schedule())
 
-        xs = keep.tile([P, 8], F32, name="xs")
+        x_scales = keep.tile([P, GROUPS * PACK], F32, name="x_scales")
         nc.scalar.dma_start(
-            out=xs[:].rearrange("p (g j) -> p g j", j=4),
-            in_=x_scale.rearrange("o (g p j) a b -> p (o g) (j a b)", p=P, j=4),
+            out=x_scales[:].rearrange("p (g j) -> p g j", j=PACK),
+            in_=x_scale.rearrange("o (g p j) a b -> p (o g) (j a b)", p=P, j=PACK),
         )
-        xbs = {}
-        for n in range(N):
-            for g in range(2):
-                xbs[n, g] = xb_pool.tile([P, 4, 2, H], U8, name="xb")
 
-        def load(n, g, ths):
-            src = x_bytes[n, 512 * g : 512 * (g + 1)].rearrange("(p j) (h t) v -> p j h (t v)", j=4, h=2)
-            if len(ths) == 2:
+        byte_planes = {}
+
+        def pass_bytes(n, g):
+            rows = x_bytes[n, P * PACK * g : P * PACK * (g + 1)]
+            return rows.rearrange("(p j) (h t) v -> p j h (t v)", j=PACK, h=2)
+
+        def load_half(n, h, g):
+            t = first_bytes.tile([P, PACK, COLS], U8, name="half_bytes")
+            nc.sync.dma_start(out=t[:], in_=pass_bytes(n, g)[:, :, h, :])
+            for j in range(PACK):
+                byte_planes[2 * n + h, g, j] = t[:, j, :]
+
+        def load_sample(n):
+            for g in range(GROUPS):
+                t = more_bytes.tile([P, PACK, 2, COLS], U8, name="sample_bytes")
                 nc.sync.dma_start(
-                    out=xbs[n, g][:].rearrange("p j h w -> p (j h w)"), in_=src.rearrange("p j h w -> p (j h w)")
+                    out=t[:].rearrange("p j h w -> p (j h w)"),
+                    in_=pass_bytes(n, g).rearrange("p j h w -> p (j h w)"),
                 )
-            else:
-                nc.sync.dma_start(out=xbs[n, g][:, :, ths[0], :], in_=src[:, :, ths[0], :])
+                for h in range(2):
+                    for j in range(PACK):
+                        byte_planes[2 * n + h, g, j] = t[:, j, h, :]
 
-        load(0, 0, [0])
-        load(0, 1, [0])
+        load_half(0, 0, 0)
+        load_half(0, 0, 1)
 
-        wsc = keep.tile([P, IC], U8, name="wsc", align_bytes=64)
-        nc.vector.memset(wsc[:].bitcast(I32), 0)
-        dummy = keep.tile([P, 1], F32, name="dummy")
-        nc.vector.memset(dummy[:], 0.0)
-        brow = keep.tile([P, P], BF16, name="brow", align_bytes=64)
-        nc.vector.memset(brow[:], 0.0)
-        nc.scalar.activation(out=dummy[:], in_=dummy[:], func=ACT.Tanh)
-        for op, src in enumerate((Wa_scales, Wb_scales)):
+        w_scales = keep.tile([P, IC], U8, name="w_scales", align_bytes=64)
+        nc.vector.memset(w_scales[:].bitcast(I32), 0)
+        bias_rows = keep.tile([P, P], BF16, name="bias_rows", align_bytes=64)
+        nc.vector.memset(bias_rows[:], 0.0)
+        identity = keep.tile([P, P], BF16, name="identity", align_bytes=64)
+        make_identity(nc, identity[:])
+        nc.gpsimd.dma_start(out=bias_rows[0:QUARTERS, :], in_=ba.rearrange("(m p) -> m p", p=P))
+        nc.gpsimd.dma_start(out=bias_rows[QUARTERS : 2 * QUARTERS, :], in_=bb.rearrange("(m p) -> m p", p=P))
+        first_tanh = keep.tile([P, 1], F32, name="first_tanh")
+        nc.vector.memset(first_tanh[:], 0.0)
+        nc.scalar.activation(out=first_tanh[:], in_=first_tanh[:], func=ACT.Tanh)
+
+        w_words = [keep.tile([P, GROUPS, IC * PACK], U8, name="w_words%d" % r, align_bytes=64) for r in range(2)]
+
+        def load_w_scales(r):
+            src = (Wa_scales, Wb_scales)[r]
             for q in range(4):
-                r = 32 * q + 8 * op
-                nc.sync.dma_start(out=wsc[r : r + 8, :].bitcast(I32), in_=src[:, 4 * q : 4 * q + 4, :].bitcast(I32))
-        wcodes = []
-        for op, src in enumerate((Wa_words, Wb_words)):
-            w = keep.tile([P, 2, IC * 4], U8, name="w%d" % op, align_bytes=64)
-            nc.sync.dma_start(out=w[:], in_=src.rearrange("g p n t -> p g (n t)"))
-            wcodes.append(w)
-        load(0, 0, [1])
-        load(0, 1, [1])
+                row = 32 * q + 8 * r
+                nc.sync.dma_start(
+                    out=w_scales[row : row + 8, :].bitcast(I32), in_=src[:, 4 * q : 4 * q + 4, :].bitcast(I32)
+                )
 
-        ident = keep.tile([P, P], BF16, name="ident", align_bytes=64)
-        make_identity(nc, ident[:])
-        nc.scalar.dma_start(out=brow[0:4, :], in_=ba.rearrange("(m p) -> m p", p=P))
-        nc.scalar.dma_start(out=brow[4:8, :], in_=bb.rearrange("(m p) -> m p", p=P))
+        def load_w_words(r):
+            nc.sync.dma_start(out=w_words[r][:], in_=(Wa_words, Wb_words)[r].rearrange("g p n t -> p g (n t)"))
+
+        load_w_scales(0)
+        load_w_words(0)
+        load_half(0, 1, 0)
+        load_half(0, 1, 1)
+        load_w_scales(1)
+        load_w_words(1)
+        load_sample(1)
         a_raw = keep.tile([P, V], BF16, name="a_raw")
-        nc.scalar.dma_start(out=a_raw[:], in_=A[0])
-        al_raw = keep.tile([P, 1], BF16, name="al_raw")
-        nc.scalar.dma_start(out=al_raw[:], in_=alpha.partition_broadcast(P))
-        for n in range(1, N):
-            load(n, 0, [0, 1])
-            load(n, 1, [0, 1])
+        nc.sync.dma_start(out=a_raw[:], in_=A[0])
+        alpha_raw = keep.tile([P, 1], BF16, name="alpha_raw")
+        nc.sync.dma_start(out=alpha_raw[:], in_=alpha.partition_broadcast(P))
 
         planes = {}
         grouped = {}
-        xq = {}
-        units = [(n, th) for n in range(N) for th in range(2)]
-        s_share = [4, 6, 3, 3, 3, 3, 3, 2]
+        x_codes = {}
 
-        def on_scalar(u, g, j):
-            return j < (s_share[u] + 1 - g) // 2
+        def on_scalar(i, g, j):
+            return j < (SCALAR_PLANES[i] + 1 - g) // 2
 
-        def widen(u, g, j):
-            n, th = units[u]
-            if (u, g) not in planes:
-                planes[u, g] = pl_pool.tile([P, 4, H], BF16, name="planes", align_bytes=64)
-            src = xbs[n, g][:, j, th, :].bitcast(FP8)
-            dst = planes[u, g][:, j, :]
-            sc = xs[:, 4 * g + j : 4 * g + j + 1]
-            if on_scalar(u, g, j):
-                nc.scalar.activation(out=dst, in_=src, func=ACT.Copy, scale=sc)
+        def planes_of(i, scalar):
+            return [(i, g, j) for g in range(GROUPS) for j in range(PACK) if on_scalar(i, g, j) == scalar]
+
+        def widen(i, g, j):
+            if (i, g) not in planes:
+                planes[i, g] = plane_pool.tile([P, PACK, COLS], BF16, name="plane", align_bytes=64)
+            dst = planes[i, g][:, j, :]
+            src = byte_planes[i, g, j].bitcast(FP8)
+            scale = x_scales[:, PACK * g + j : PACK * g + j + 1]
+            if on_scalar(i, g, j):
+                nc.scalar.activation(out=dst, in_=src, func=ACT.Copy, scale=scale)
             else:
-                nc.vector.tensor_scalar(out=dst, in0=src, scalar1=sc, scalar2=None, op0=ALU.mult)
+                nc.vector.tensor_scalar(out=dst, in0=src, scalar1=scale, scalar2=None, op0=ALU.mult)
 
-        def widen_on(u, scalar):
-            return [(u, g, j) for g in range(2) for j in range(4) if on_scalar(u, g, j) == scalar]
-
-        def interleave(u, g):
-            t = gr_pool.tile([P, H, 4], BF16, name="grouped", align_bytes=64)
-            grouped[u, g] = t
+        def group(i, g):
+            t = group_pool.tile([P, COLS, PACK], BF16, name="grouped_x", align_bytes=64)
             nc.vector.tensor_copy(
                 out=t[:].rearrange("p (c i) j -> p c j i", i=4),
-                in_=planes[u, g][:].rearrange("p j (c i) -> p c j i", i=4),
+                in_=planes[i, g][:].rearrange("p j (c i) -> p c j i", i=4),
             )
+            grouped[i, g] = t
 
-        def quant(u, g):
-            cw = codes.tile([P, H], U32, name="cw", align_bytes=64)
-            cs = codes.tile([P, H], U8, name="cs", align_bytes=64)
+        def quantise_x(i, g):
+            words = codes.tile([P, COLS], U32, name="x_words", align_bytes=64)
+            scales = codes.tile([P, COLS], U8, name="x_word_scales", align_bytes=64)
             nc.vector.quantize_mx(
-                out=cw[:].bitcast(FP8X4), scales=cs[:], in_=grouped[u, g][:].rearrange("p w j -> p (w j)")
+                out=words[:].bitcast(FP8X4), scales=scales[:], in_=grouped[i, g][:].rearrange("p w j -> p (w j)")
             )
-            xq[u, g] = (cw, cs)
+            x_codes[i, g] = (words, scales)
 
-        ys = {}
-        xt = {}
+        def make_x(i, between, before_last):
+            for plane in planes_of(i, False):
+                widen(*plane)
+            group(i, 0)
+            for work in between:
+                work()
+            group(i, 1)
+            quantise_x(i, 0)
+            for work in before_last:
+                work()
+            quantise_x(i, 1)
 
-        def project(u, m, op):
-            n, th = units[u]
-            if op == 0:
-                ys[u, m] = ypool.tile([P, 2, H], BF16, name="y", align_bytes=64)
-            bank = psum.tile([P, H], F32, name="bank")
-            for g in range(2):
-                cw, cs = xq[u, g]
+        rows = {}
+
+        def project(i, k):
+            m, r = k // 2, k % 2
+            bank = psum.tile([P, COLS], F32, name="bank")
+            for g in range(GROUPS):
+                words, scales = x_codes[i, g]
                 nc.tensor.matmul_mx(
                     out=bank[:],
-                    lhsT=wcodes[op][:, g, 512 * m : 512 * (m + 1)].bitcast(FP8X4),
-                    lhsT_scale=wsc[4 * (2 * op + g) : P, 128 * m : 128 * (m + 1)],
-                    rhs=cw[:].bitcast(FP8X4),
-                    rhs_scale=cs[:],
+                    lhsT=w_words[r][:, g, P * PACK * m : P * PACK * (m + 1)].bitcast(FP8X4),
+                    lhsT_scale=w_scales[4 * (2 * r + g) : P, P * m : P * (m + 1)],
+                    rhs=words[:].bitcast(FP8X4),
+                    rhs_scale=scales[:],
                     start=(g == 0),
-                    stop=(g == 1),
+                    stop=(g == GROUPS - 1),
                 )
-            dst = ys[u, m][:, op, :].rearrange("p (v j) -> p v j", j=4)
-            src = bank[:].rearrange("p (j v) -> p v j", j=4)
-            b = bias[:, 4 * op + m : 4 * op + m + 1]
-            if u == len(units) - 1 and op == 1:
-                nc.vector.tensor_scalar(out=dst, in0=src, scalar1=b, scalar2=None, op0=ALU.add)
+            if r == 0:
+                rows[i, m] = row_pool.tile([P, 2, COLS], BF16, name="row", align_bytes=64)
+            dst = rows[i, m][:, r, :].rearrange("p (v u) -> p v u", u=4)
+            src = bank[:].rearrange("p (u v) -> p v u", u=4)
+            bias = biases[:, QUARTERS * r + m : QUARTERS * r + m + 1]
+            if (i, k) in VECTOR_BANKS:
+                nc.vector.tensor_scalar(out=dst, in0=src, scalar1=bias, scalar2=None, op0=ALU.add)
             else:
-                nc.scalar.activation(out=dst, in_=src, func=ACT.Identity, bias=b)
+                nc.scalar.activation(out=dst, in_=src, func=ACT.Identity, bias=bias)
 
-        def swap(u, m):
-            n, th = units[u]
-            if th == 0:
-                xt[n, m] = xpool.tile([P, 2, 2 * H], BF16, name="xt", align_bytes=64)
-            for hh in range(2):
+        quarters = {}
+
+        def exchange(i, m):
+            n, h = i // 2, i % 2
+            if h == 0:
+                quarters[n, m] = quarter_pool.tile([P, 2, 2 * COLS], BF16, name="quarter", align_bytes=64)
+            for b in range(2):
                 nc.sync.dma_start(
-                    out=xt[n, m][th:P:2, hh, :],
-                    in_=ys[u, m][64 * hh : 64 * hh + 64, :, :].rearrange("p o w -> p (o w)"),
+                    out=quarters[n, m][h:P:2, b, :],
+                    in_=rows[i, m][64 * b : 64 * b + 64, :, :].rearrange("p r w -> p (r w)"),
                 )
 
-        qc = {}
+        q_codes = {}
 
-        def requant(n, m):
-            cw = codes.tile([P, 2, 2 * V], U32, name="ew", align_bytes=64)
-            cs = codes.tile([P, 2, 2 * V], U8, name="es", align_bytes=64)
-            nc.vector.quantize_mx(
-                out=cw[:].rearrange("p h w -> p (h w)").bitcast(FP8X4),
-                scales=cs[:].rearrange("p h w -> p (h w)"),
-                in_=xt[n, m][:].rearrange("p h w -> p (h w)"),
-            )
-            qc[n, m] = (cw, cs)
-
-        gps = {}
-
-        def product(n, m):
-            if m == 0:
-                gps[n] = psum2.tile([P, V], F32, name="gps")
-            cw, cs = qc[n, m]
-            for hh in range(2):
-                nc.tensor.matmul_mx(
-                    out=gps[n][:],
-                    lhsT=cw[:, hh, 0:V].bitcast(FP8X4),
-                    lhsT_scale=cs[:, hh, 0:V],
-                    rhs=cw[:, hh, V : 2 * V].bitcast(FP8X4),
-                    rhs_scale=cs[:, hh, V : 2 * V],
-                    start=(m == 0 and hh == 0),
-                    stop=(m == 3 and hh == 1),
-                )
-
-        def finish(n):
-            t = small.tile([P, V], F32, name="t")
-            nc.scalar.activation(out=t[:], in_=gps[n][:], func=ACT.Tanh, scale=1.0 / (IC * T))
-            nz = small.tile([P, V], F32, name="nz")
-            nc.vector.scalar_tensor_tensor(
-                out=nz[:], in0=t[:], scalar=neg_al[:, 0:1], in1=neg_a[:], op0=ALU.mult, op1=ALU.add
-            )
-            mn = small.tile([P, 1], F32, name="mn")
-            nc.vector.tensor_reduce(out=mn[:], in_=nz[:], axis=AX.X, op=ALU.min)
-            e = small.tile([P, V], F32, name="e")
-            tot = small.tile([P, 1], F32, name="tot")
-            nc.scalar.activation(out=e[:], in_=nz[:], func=ACT.Exp, scale=-1.0, bias=mn[:, 0:1], accum_out=tot[:])
-            rec = small.tile([P, 1], F32, name="rec")
-            nc.vector.reciprocal(out=rec[:], in_=tot[:])
-            o = small.tile([P, V], F32, name="o")
-            nc.vector.tensor_scalar(out=o[:], in0=e[:], scalar1=rec[:, 0:1], scalar2=None, op0=ALU.mult)
-            nc.sync.dma_start(out=out[n], in_=o[:])
-
-        for u in range(2):
-            for a in widen_on(u, True):
-                widen(*a)
-        for a in widen_on(0, False):
-            widen(*a)
-        interleave(0, 0)
-        interleave(0, 1)
-        quant(0, 0)
-        bias = keep.tile([P, 8], F32, name="bias")
-        tb = psum.tile([P, P], BF16, name="bank")
-        nc.tensor.transpose(tb[:], brow[:], ident[:])
-        nc.vector.tensor_copy(out=bias[:], in_=tb[:, 0:8])
-        quant(0, 1)
-        neg_a = keep.tile([P, V], F32, name="neg_a")
-        nc.vector.tensor_scalar(out=neg_a[:], in0=a_raw[:], scalar1=-1.0, scalar2=None, op0=ALU.mult)
-        neg_al = keep.tile([P, 1], F32, name="neg_al")
-        nc.vector.tensor_scalar(out=neg_al[:], in0=al_raw[:], scalar1=-1.0, scalar2=None, op0=ALU.mult)
-
-        last = len(units) - 1
-        ready = []
-        for u, (n, th) in enumerate(units):
-            s_work = widen_on(u + 2, True) if u + 2 <= last else []
-            todo = [(n - 1, 2 * th), (n - 1, 2 * th + 1)] if n > 0 else []
-            if u < last:
-                for a in widen_on(u + 1, False):
-                    widen(*a)
-                interleave(u + 1, 0)
-                if todo:
-                    requant(*todo[0])
-                interleave(u + 1, 1)
-                quant(u + 1, 0)
-                if todo:
-                    requant(*todo[1])
-                quant(u + 1, 1)
+        def quantise_quarter(n, m):
+            words = codes.tile([P, 2, 2 * V], U32, name="q_words", align_bytes=64)
+            scales = codes.tile([P, 2, 2 * V], U8, name="q_word_scales", align_bytes=64)
+            if (n, m) == (N - 1, QUARTERS - 1):
+                for b in range(2):
+                    nc.vector.quantize_mx(
+                        out=words[:, b, :].bitcast(FP8X4), scales=scales[:, b, :], in_=quarters[n, m][:, b, :]
+                    )
             else:
-                for a in todo:
-                    requant(*a)
-            done = None
-            for k in range(8):
-                m, op = k // 2, k % 2
-                project(u, m, op)
-                if op == 1:
-                    swap(u, m)
-                if k in (1, 3, 5) and s_work:
-                    widen(*s_work.pop(0))
-                if k == 3:
-                    for a in ready:
-                        product(*a)
-                        if a[1] == 3:
-                            done = a[0]
-                    ready = todo
-            for a in s_work:
-                widen(*a)
-            if done is not None:
-                finish(done)
-        for a in ready:
-            product(*a)
-        finish(N - 2)
-        for m in range(4):
-            requant(N - 1, m)
-            product(N - 1, m)
-        finish(N - 1)
+                nc.vector.quantize_mx(
+                    out=words[:].rearrange("p b w -> p (b w)").bitcast(FP8X4),
+                    scales=scales[:].rearrange("p b w -> p (b w)"),
+                    in_=quarters[n, m][:].rearrange("p b w -> p (b w)"),
+                )
+            q_codes[n, m] = (words, scales)
+
+        g_banks = {}
+        done_parts = {}
+
+        def multiply_quarter(n, m):
+            if m == 0:
+                g_banks[n] = psum_g.tile([P, V], F32, name="g_bank")
+            words, scales = q_codes[n, m]
+            for b in range(2):
+                nc.tensor.matmul_mx(
+                    out=g_banks[n][:],
+                    lhsT=words[:, b, 0:V].bitcast(FP8X4),
+                    lhsT_scale=scales[:, b, 0:V],
+                    rhs=words[:, b, V : 2 * V].bitcast(FP8X4),
+                    rhs_scale=scales[:, b, V : 2 * V],
+                    start=(m == 0 and b == 0),
+                    stop=(m == QUARTERS - 1 and b == 1),
+                )
+            if m == QUARTERS - 1:
+                done_parts[n] = 0
+
+        end_tiles = {}
+
+        def end_tanh(n):
+            t = ends.tile([P, V], F32, name="tanh_g")
+            nc.scalar.activation(out=t[:], in_=g_banks[n][:], func=ACT.Tanh, scale=1.0 / (IC * T))
+            end_tiles[n] = (t,)
+
+        def end_sum(n):
+            (t,) = end_tiles[n]
+            z = ends.tile([P, V], F32, name="z")
+            nc.vector.scalar_tensor_tensor(
+                out=z[:], in0=t[:], scalar=minus_alpha[:, 0:1], in1=minus_a[:], op0=ALU.mult, op1=ALU.add
+            )
+            end_tiles[n] = (z,)
+
+        def end_least(n):
+            (z,) = end_tiles[n]
+            least = ends.tile([P, 1], F32, name="least")
+            nc.vector.tensor_reduce(out=least[:], in_=z[:], axis=AX.X, op=ALU.min)
+            end_tiles[n] = (z, least)
+
+        def end_exp(n):
+            z, least = end_tiles[n]
+            e = ends.tile([P, V], F32, name="exp_z")
+            total = ends.tile([P, 1], F32, name="total")
+            nc.scalar.activation(
+                out=e[:], in_=z[:], func=ACT.Exp, scale=-1.0, bias=least[:, 0:1], accum_out=total[:]
+            )
+            end_tiles[n] = (e, total)
+
+        def end_reciprocal(n):
+            e, total = end_tiles[n]
+            inverse = ends.tile([P, 1], F32, name="inverse")
+            nc.vector.reciprocal(out=inverse[:], in_=total[:])
+            end_tiles[n] = (e, inverse)
+
+        def end_store(n):
+            e, inverse = end_tiles[n]
+            result = ends.tile([P, V], F32, name="result")
+            nc.vector.tensor_scalar(out=result[:], in0=e[:], scalar1=inverse[:, 0:1], scalar2=None, op0=ALU.mult)
+            nc.sync.dma_start(out=out[n], in_=result[:])
+
+        END_PARTS = [
+            ("scalar", end_tanh),
+            ("vector", end_sum),
+            ("vector", end_least),
+            ("scalar", end_exp),
+            ("vector", end_reciprocal),
+            ("vector", end_store),
+        ]
+
+        def advance(engine):
+            for n in sorted(done_parts):
+                if done_parts[n] < len(END_PARTS) and END_PARTS[done_parts[n]][0] == engine:
+                    END_PARTS[done_parts[n]][1](n)
+                    done_parts[n] += 1
+
+        for i in range(2):
+            for plane in planes_of(i, True):
+                widen(*plane)
+        make_x(0, [], [])
+        biases = keep.tile([P, 2 * QUARTERS], F32, name="biases")
+        turned = psum.tile([P, P], BF16, name="bank")
+        nc.tensor.transpose(turned[:], bias_rows[:], identity[:])
+        nc.vector.tensor_copy(out=biases[:], in_=turned[:, 0 : 2 * QUARTERS])
+
+        minus_a = keep.tile([P, V], F32, name="minus_a")
+        minus_alpha = keep.tile([P, 1], F32, name="minus_alpha")
+        waiting = []
+        quantised = []
+
+        def multiply_quantised(keep_back):
+            while len(quantised) > keep_back:
+                multiply_quarter(*quantised.pop(0))
+
+        def take_quarter():
+            quarter = waiting.pop(0)
+            quantise_quarter(*quarter)
+            quantised.append(quarter)
+
+        for i in range(HALVES):
+            scalar_planes = planes_of(i + 2, True) if i + 2 <= LAST else []
+            if i < 2:
+                load_sample(i + 2)
+            if i == 2:
+                for dst, src in ((minus_a, a_raw), (minus_alpha, alpha_raw)):
+                    nc.vector.tensor_scalar(out=dst[:], in0=src[:], scalar1=-1.0, scalar2=None, op0=ALU.mult)
+            beside = QUARTERS_BESIDE[i]
+            earlier = len(quantised)
+            if i < LAST:
+                between = [lambda: advance("vector")] + [take_quarter] * min(beside, 1)
+                before_last = [take_quarter] * (beside - 1) + [lambda: advance("vector")]
+                make_x(i + 1, between, before_last)
+            for k in range(2 * QUARTERS):
+                project(i, k)
+                if k % 2 == 1:
+                    exchange(i, k // 2)
+                if i == LAST and k % 2 == 1:
+                    multiply_quantised(2)
+                    for step in range(min(2, len(waiting))):
+                        advance("vector")
+                        take_quarter()
+                if k in (1, 3, 5) and scalar_planes:
+                    widen(*scalar_planes.pop(0))
+                if k == 5 and i < LAST:
+                    multiply_quantised(len(quantised) - earlier)
+                if k == 2 * QUARTERS - 1:
+                    advance("scalar")
+            for plane in scalar_planes:
+                widen(*plane)
+            if i % 2 == 1:
+                waiting.extend((i // 2, m) for m in range(QUARTERS))
+
+        while waiting:
+            last_sample = waiting[0][0] == N - 1
+            take_quarter()
+            multiply_quantised(0)
+            if last_sample and len(waiting) > 0:
+                advance("scalar")
+                advance("vector")
+        for step in END_PARTS:
+            advance("scalar")
+            advance("vector")

from contextlib import ExitStack

import concourse.mybir as mybir
from concourse.masks import make_identity

N, C, T, V, IC = 4, 1024, 8, 128, 512

F32 = mybir.dt.float32
BF16 = mybir.dt.bfloat16
U32 = mybir.dt.uint32
I32 = mybir.dt.int32
U8 = mybir.dt.uint8
FP8 = mybir.dt.float8_e4m3fn
FP8X4 = mybir.dt.float8_e4m3fn_x4
ACT = mybir.ActivationFunctionType
ALU = mybir.AluOpType
AX = mybir.AxisListType

FLOPS = 2 * 2 * N * IC * C * T * V + N * 2 * V * V * IC * T

P = 128
PACK = 4
GROUPS = C // (P * PACK)
COLS = T // 2 * V
HALVES = 2 * N
LAST = HALVES - 1
QUARTERS = IC // P

SCALAR_PLANES = [4, 6] + [2] * (HALVES - 2)
VECTOR_BANKS = [(6, 4)]
QUARTERS_BESIDE = [0, 0, 1, 1, 0, 2, 0, 0]


def tile_adaptivegraphconstruction_t_w8_kernel(
    tc, x_bytes, x_scale, Wa_words, Wa_scales, ba, Wb_words, Wb_scales, bb, A, alpha, out
):
    nc = tc.nc
    with ExitStack() as ctx:
        keep = ctx.enter_context(tc.tile_pool(name="keep", bufs=1))
        first_bytes = ctx.enter_context(tc.tile_pool(name="first_bytes", bufs=2 * GROUPS))
        more_bytes = ctx.enter_context(tc.tile_pool(name="more_bytes", bufs=(N - 1) * GROUPS))
        plane_pool = ctx.enter_context(tc.tile_pool(name="plane_pool", bufs=3 * GROUPS))
        group_pool = ctx.enter_context(tc.tile_pool(name="group_pool", bufs=2 * GROUPS))
        codes = ctx.enter_context(tc.tile_pool(name="codes", bufs=3 * GROUPS))
        row_pool = ctx.enter_context(tc.tile_pool(name="row_pool", bufs=HALVES * QUARTERS))
        quarter_pool = ctx.enter_context(tc.tile_pool(name="quarter_pool", bufs=(N - 1) * QUARTERS))
        ends = ctx.enter_context(tc.tile_pool(name="ends", bufs=N))
        psum = ctx.enter_context(tc.psum_pool(name="psum", bufs=6))
        psum_g = ctx.enter_context(tc.psum_pool(name="psum_g", bufs=2))
        ctx.enter_context(tc.manual_schedule())

        x_scales = keep.tile([P, GROUPS * PACK], F32, name="x_scales")
        nc.scalar.dma_start(
            out=x_scales[:].rearrange("p (g j) -> p g j", j=PACK),
            in_=x_scale.rearrange("o (g p j) a b -> p (o g) (j a b)", p=P, j=PACK),
        )

        byte_planes = {}

        def pass_bytes(n, g):
            rows = x_bytes[n, P * PACK * g : P * PACK * (g + 1)]
            return rows.rearrange("(p j) (h t) v -> p j h (t v)", j=PACK, h=2)

        def load_half(n, h, g):
            t = first_bytes.tile([P, PACK, COLS], U8, name="half_bytes")
            nc.sync.dma_start(out=t[:], in_=pass_bytes(n, g)[:, :, h, :])
            for j in range(PACK):
                byte_planes[2 * n + h, g, j] = t[:, j, :]

        def load_sample(n):
            for g in range(GROUPS):
                t = more_bytes.tile([P, PACK, 2, COLS], U8, name="sample_bytes")
                nc.sync.dma_start(
                    out=t[:].rearrange("p j h w -> p (j h w)"),
                    in_=pass_bytes(n, g).rearrange("p j h w -> p (j h w)"),
                )
                for h in range(2):
                    for j in range(PACK):
                        byte_planes[2 * n + h, g, j] = t[:, j, h, :]

        load_half(0, 0, 0)
        load_half(0, 0, 1)

        w_scales = keep.tile([P, IC], U8, name="w_scales", align_bytes=64)
        nc.vector.memset(w_scales[:].bitcast(I32), 0)
        bias_rows = keep.tile([P, P], BF16, name="bias_rows", align_bytes=64)
        nc.vector.memset(bias_rows[:], 0.0)
        identity = keep.tile([P, P], BF16, name="identity", align_bytes=64)
        make_identity(nc, identity[:])
        nc.gpsimd.dma_start(out=bias_rows[0:QUARTERS, :], in_=ba.rearrange("(m p) -> m p", p=P))
        nc.gpsimd.dma_start(out=bias_rows[QUARTERS : 2 * QUARTERS, :], in_=bb.rearrange("(m p) -> m p", p=P))
        first_tanh = keep.tile([P, 1], F32, name="first_tanh")
        nc.vector.memset(first_tanh[:], 0.0)
        nc.scalar.activation(out=first_tanh[:], in_=first_tanh[:], func=ACT.Tanh)

        w_words = [keep.tile([P, GROUPS, IC * PACK], U8, name="w_words%d" % r, align_bytes=64) for r in range(2)]

        def load_w_scales(r):
            src = (Wa_scales, Wb_scales)[r]
            for q in range(4):
                row = 32 * q + 8 * r
                nc.sync.dma_start(
                    out=w_scales[row : row + 8, :].bitcast(I32), in_=src[:, 4 * q : 4 * q + 4, :].bitcast(I32)
                )

        def load_w_words(r):
            nc.sync.dma_start(out=w_words[r][:], in_=(Wa_words, Wb_words)[r].rearrange("g p n t -> p g (n t)"))

        load_w_scales(0)
        load_w_words(0)
        load_half(0, 1, 0)
        load_half(0, 1, 1)
        load_w_scales(1)
        load_w_words(1)
        load_sample(1)
        a_raw = keep.tile([P, V], BF16, name="a_raw")
        nc.sync.dma_start(out=a_raw[:], in_=A[0])
        alpha_raw = keep.tile([P, 1], BF16, name="alpha_raw")
        nc.sync.dma_start(out=alpha_raw[:], in_=alpha.partition_broadcast(P))

        planes = {}
        grouped = {}
        x_codes = {}

        def on_scalar(i, g, j):
            return j < (SCALAR_PLANES[i] + 1 - g) // 2

        def planes_of(i, scalar):
            return [(i, g, j) for g in range(GROUPS) for j in range(PACK) if on_scalar(i, g, j) == scalar]

        def widen(i, g, j):
            if (i, g) not in planes:
                planes[i, g] = plane_pool.tile([P, PACK, COLS], BF16, name="plane", align_bytes=64)
            dst = planes[i, g][:, j, :]
            src = byte_planes[i, g, j].bitcast(FP8)
            scale = x_scales[:, PACK * g + j : PACK * g + j + 1]
            if on_scalar(i, g, j):
                nc.scalar.activation(out=dst, in_=src, func=ACT.Copy, scale=scale)
            else:
                nc.vector.tensor_scalar(out=dst, in0=src, scalar1=scale, scalar2=None, op0=ALU.mult)

        def group(i, g):
            t = group_pool.tile([P, COLS, PACK], BF16, name="grouped_x", align_bytes=64)
            nc.vector.tensor_copy(
                out=t[:].rearrange("p (c i) j -> p c j i", i=4),
                in_=planes[i, g][:].rearrange("p j (c i) -> p c j i", i=4),
            )
            grouped[i, g] = t

        def quantise_x(i, g):
            words = codes.tile([P, COLS], U32, name="x_words", align_bytes=64)
            scales = codes.tile([P, COLS], U8, name="x_word_scales", align_bytes=64)
            nc.vector.quantize_mx(
                out=words[:].bitcast(FP8X4), scales=scales[:], in_=grouped[i, g][:].rearrange("p w j -> p (w j)")
            )
            x_codes[i, g] = (words, scales)

        def make_x(i, between, before_last):
            for plane in planes_of(i, False):
                widen(*plane)
            group(i, 0)
            for work in between:
                work()
            group(i, 1)
            quantise_x(i, 0)
            for work in before_last:
                work()
            quantise_x(i, 1)

        rows = {}

        def project(i, k):
            m, r = k // 2, k % 2
            bank = psum.tile([P, COLS], F32, name="bank")
            for g in range(GROUPS):
                words, scales = x_codes[i, g]
                nc.tensor.matmul_mx(
                    out=bank[:],
                    lhsT=w_words[r][:, g, P * PACK * m : P * PACK * (m + 1)].bitcast(FP8X4),
                    lhsT_scale=w_scales[4 * (2 * r + g) : P, P * m : P * (m + 1)],
                    rhs=words[:].bitcast(FP8X4),
                    rhs_scale=scales[:],
                    start=(g == 0),
                    stop=(g == GROUPS - 1),
                )
            if r == 0:
                rows[i, m] = row_pool.tile([P, 2, COLS], BF16, name="row", align_bytes=64)
            dst = rows[i, m][:, r, :].rearrange("p (v u) -> p v u", u=4)
            src = bank[:].rearrange("p (u v) -> p v u", u=4)
            bias = biases[:, QUARTERS * r + m : QUARTERS * r + m + 1]
            if (i, k) in VECTOR_BANKS:
                nc.vector.tensor_scalar(out=dst, in0=src, scalar1=bias, scalar2=None, op0=ALU.add)
            else:
                nc.scalar.activation(out=dst, in_=src, func=ACT.Identity, bias=bias)

        quarters = {}

        def exchange(i, m):
            n, h = i // 2, i % 2
            if h == 0:
                quarters[n, m] = quarter_pool.tile([P, 2, 2 * COLS], BF16, name="quarter", align_bytes=64)
            for b in range(2):
                nc.sync.dma_start(
                    out=quarters[n, m][h:P:2, b, :],
                    in_=rows[i, m][64 * b : 64 * b + 64, :, :].rearrange("p r w -> p (r w)"),
                )

        q_codes = {}

        def quantise_quarter(n, m):
            words = codes.tile([P, 2, 2 * V], U32, name="q_words", align_bytes=64)
            scales = codes.tile([P, 2, 2 * V], U8, name="q_word_scales", align_bytes=64)
            if (n, m) == (N - 1, QUARTERS - 1):
                for b in range(2):
                    nc.vector.quantize_mx(
                        out=words[:, b, :].bitcast(FP8X4), scales=scales[:, b, :], in_=quarters[n, m][:, b, :]
                    )
            else:
                nc.vector.quantize_mx(
                    out=words[:].rearrange("p b w -> p (b w)").bitcast(FP8X4),
                    scales=scales[:].rearrange("p b w -> p (b w)"),
                    in_=quarters[n, m][:].rearrange("p b w -> p (b w)"),
                )
            q_codes[n, m] = (words, scales)

        g_banks = {}
        done_parts = {}

        def multiply_quarter(n, m):
            if m == 0:
                g_banks[n] = psum_g.tile([P, V], F32, name="g_bank")
            words, scales = q_codes[n, m]
            for b in range(2):
                nc.tensor.matmul_mx(
                    out=g_banks[n][:],
                    lhsT=words[:, b, 0:V].bitcast(FP8X4),
                    lhsT_scale=scales[:, b, 0:V],
                    rhs=words[:, b, V : 2 * V].bitcast(FP8X4),
                    rhs_scale=scales[:, b, V : 2 * V],
                    start=(m == 0 and b == 0),
                    stop=(m == QUARTERS - 1 and b == 1),
                )
            if m == QUARTERS - 1:
                done_parts[n] = 0

        end_tiles = {}

        def end_tanh(n):
            t = ends.tile([P, V], F32, name="tanh_g")
            nc.scalar.activation(out=t[:], in_=g_banks[n][:], func=ACT.Tanh, scale=1.0 / (IC * T))
            end_tiles[n] = (t,)

        def end_sum(n):
            (t,) = end_tiles[n]
            z = ends.tile([P, V], F32, name="z")
            nc.vector.scalar_tensor_tensor(
                out=z[:], in0=t[:], scalar=minus_alpha[:, 0:1], in1=minus_a[:], op0=ALU.mult, op1=ALU.add
            )
            end_tiles[n] = (z,)

        def end_least(n):
            (z,) = end_tiles[n]
            least = ends.tile([P, 1], F32, name="least")
            nc.vector.tensor_reduce(out=least[:], in_=z[:], axis=AX.X, op=ALU.min)
            end_tiles[n] = (z, least)

        def end_exp(n):
            z, least = end_tiles[n]
            e = ends.tile([P, V], F32, name="exp_z")
            total = ends.tile([P, 1], F32, name="total")
            nc.scalar.activation(
                out=e[:], in_=z[:], func=ACT.Exp, scale=-1.0, bias=least[:, 0:1], accum_out=total[:]
            )
            end_tiles[n] = (e, total)

        def end_reciprocal(n):
            e, total = end_tiles[n]
            inverse = ends.tile([P, 1], F32, name="inverse")
            nc.vector.reciprocal(out=inverse[:], in_=total[:])
            end_tiles[n] = (e, inverse)

        def end_store(n):
            e, inverse = end_tiles[n]
            result = ends.tile([P, V], F32, name="result")
            nc.vector.tensor_scalar(out=result[:], in0=e[:], scalar1=inverse[:, 0:1], scalar2=None, op0=ALU.mult)
            nc.sync.dma_start(out=out[n], in_=result[:])

        END_PARTS = [
            ("scalar", end_tanh),
            ("vector", end_sum),
            ("vector", end_least),
            ("scalar", end_exp),
            ("vector", end_reciprocal),
            ("vector", end_store),
        ]

        def advance(engine):
            for n in sorted(done_parts):
                if done_parts[n] < len(END_PARTS) and END_PARTS[done_parts[n]][0] == engine:
                    END_PARTS[done_parts[n]][1](n)
                    done_parts[n] += 1

        for i in range(2):
            for plane in planes_of(i, True):
                widen(*plane)
        make_x(0, [], [])
        biases = keep.tile([P, 2 * QUARTERS], F32, name="biases")
        turned = psum.tile([P, P], BF16, name="bank")
        nc.tensor.transpose(turned[:], bias_rows[:], identity[:])
        nc.vector.tensor_copy(out=biases[:], in_=turned[:, 0 : 2 * QUARTERS])

        minus_a = keep.tile([P, V], F32, name="minus_a")
        minus_alpha = keep.tile([P, 1], F32, name="minus_alpha")
        waiting = []
        quantised = []

        def multiply_quantised(keep_back):
            while len(quantised) > keep_back:
                multiply_quarter(*quantised.pop(0))

        def take_quarter():
            quarter = waiting.pop(0)
            quantise_quarter(*quarter)
            quantised.append(quarter)

        for i in range(HALVES):
            scalar_planes = planes_of(i + 2, True) if i + 2 <= LAST else []
            if i < 2:
                load_sample(i + 2)
            if i == 2:
                for dst, src in ((minus_a, a_raw), (minus_alpha, alpha_raw)):
                    nc.vector.tensor_scalar(out=dst[:], in0=src[:], scalar1=-1.0, scalar2=None, op0=ALU.mult)
            beside = QUARTERS_BESIDE[i]
            earlier = len(quantised)
            if i < LAST:
                between = [lambda: advance("vector")] + [take_quarter] * min(beside, 1)
                before_last = [take_quarter] * (beside - 1) + [lambda: advance("vector")]
                make_x(i + 1, between, before_last)
            for k in range(2 * QUARTERS):
                project(i, k)
                if k % 2 == 1:
                    exchange(i, k // 2)
                if i == LAST and k % 2 == 1:
                    multiply_quantised(2)
                    for step in range(min(2, len(waiting))):
                        advance("vector")
                        take_quarter()
                if k in (1, 3, 5) and scalar_planes:
                    widen(*scalar_planes.pop(0))
                if k == 5 and i < LAST:
                    multiply_quantised(len(quantised) - earlier)
                if k == 2 * QUARTERS - 1:
                    advance("scalar")
            for plane in scalar_planes:
                widen(*plane)
            if i % 2 == 1:
                waiting.extend((i // 2, m) for m in range(QUARTERS))

        while waiting:
            last_sample = waiting[0][0] == N - 1
            take_quarter()
            multiply_quantised(0)
            if last_sample and len(waiting) > 0:
                advance("scalar")
                advance("vector")
        for step in END_PARTS:
            advance("scalar")
            advance("vector")
